import numpy as np
import ml_dtypes


def mxq(x, axis, fmt="e4m3"):
    dtype, down = {"e4m3": (ml_dtypes.float8_e4m3fn, 7), "e5m2": (ml_dtypes.float8_e5m2, 14)}[fmt]
    v = np.moveaxis(np.asarray(x, np.float32).astype(ml_dtypes.bfloat16).astype(np.float64), axis, -1)
    blocks = v.reshape(v.shape[:-1] + (-1, 32))
    amax = np.abs(blocks).max(-1, keepdims=True)
    byte = np.maximum(np.where(amax > 0, np.frexp(amax)[1] - 1 + 127, 0) - down, 1)
    scale = np.exp2(byte - 127.0)
    codes = (blocks / scale).astype(np.float32).astype(dtype).astype(np.float64)
    return np.moveaxis((codes * scale).reshape(v.shape), -1, axis)


WIDE = False


def mx_kscale(k):
    if not WIDE:
        return np.ones(k)
    levels = np.array([10, -10, 5, -5, 0])
    a = np.random.permutation(np.resize(levels, k // 512 * 4)).reshape(k // 512, 4)
    idx = np.arange(k)
    return np.exp2(a[idx // 512, idx % 128 // 32])


BF16 = ml_dtypes.bfloat16


def bf(x):
    return np.asarray(x, np.float32).astype(BF16)


def f64(x):
    return np.asarray(x).astype(np.float64)


E2M1 = np.array([0.0, 0.5, 1.0, 1.5, 2.0, 3.0, 4.0, 6.0, -0.0, -0.5, -1.0, -1.5, -2.0, -3.0, -4.0, -6.0])


def pack_weight(w, fmt):
    k, n = w.shape
    w = f64(bf(w)).reshape(k // 32, 32, n)
    amax = np.abs(w).max(1)
    if fmt == "e4m3":
        byte = np.frexp(amax)[1] - 1 + 127 - 7
    else:
        mant, ex = np.frexp(amax / 6.0)
        byte = np.where(mant > 0.5, ex, ex - 1) + 127
    byte = np.clip(np.where(amax > 0, byte, 1), 1, 254)
    scaled = (w * np.exp2(127.0 - byte)[:, None, :]).reshape(k, n).astype(np.float32)
    by_word = np.ascontiguousarray(scaled.reshape(k // 512, 128, 4, n).transpose(0, 1, 3, 2))
    if fmt == "e4m3":
        words = by_word.astype(ml_dtypes.float8_e4m3fn).view(np.uint8)
    else:
        c = by_word.astype(ml_dtypes.float4_e2m1fn).view(np.uint8) & 0xF
        words = c[..., 0::2] | (c[..., 1::2] << 4)
    return np.ascontiguousarray(words), np.ascontiguousarray(byte.astype(np.uint8).reshape(k // 512, 16, n))


def unpack_weight(words, scales, fmt):
    g, p, n, _ = words.shape
    if fmt == "e4m3":
        vals = np.ascontiguousarray(words).view(ml_dtypes.float8_e4m3fn).astype(np.float64)
    else:
        nib = np.empty((g, p, n, 4), np.uint8)
        nib[..., 0::2] = words & 0xF
        nib[..., 1::2] = words >> 4
        vals = E2M1[nib]
    vals = vals * np.repeat(np.exp2(scales.astype(np.float64) - 127.0), 8, axis=1)[..., None]
    return vals.transpose(0, 1, 3, 2).reshape(g * 512, n)

def pack4(w):
    words, scales = pack_weight(w, "e2m1")
    return words.reshape(words.shape[0], 128, -1), scales


def unpack4(words, scales):
    return unpack_weight(words.reshape(words.shape[0], 128, -1, 2), scales, "e2m1")


B, T, C, HS, DW, DA, DV, DG = 4, 1024, 1024, 64, 128, 128, 128, 256


def sigmoid(z):
    return 1.0 / (1.0 + np.exp(-z))


def setup_inputs():
    s = mx_kscale(C)
    x = bf(np.random.standard_normal((B, T, C)) * s)
    v_first = bf(np.random.standard_normal((B, T, C)))
    x_v = bf(np.random.uniform(0.0, 1.0, C))
    Wv = np.random.standard_normal((C, C)) / np.sqrt(C) / s[None, :]
    Wv_words, Wv_scales = pack4(np.ascontiguousarray(Wv.T))
    v0 = bf(np.random.standard_normal(C))
    xv_v1 = bf(0.8 * np.random.standard_normal((B, T, DV)))
    v2 = bf(np.random.standard_normal((DV, C)) / np.sqrt(DV))
    return {
        "x": x,
        "v_first": v_first,
        "x_v": x_v,
        "Wv_words": Wv_words,
        "Wv_scales": Wv_scales,
        "v0": v0,
        "xv_v1": xv_v1,
        "v2": v2,
    }


def reference(x, v_first, x_v, Wv_words, Wv_scales, v0, xv_v1, v2):
    x = f64(x)
    xprev = np.concatenate([np.zeros_like(x[:, :1]), x[:, :-1]], axis=1)
    xx = xprev - x
    xv = x + xx * f64(x_v)
    v = mxq(xv, 2, "e4m3") @ unpack4(Wv_words, Wv_scales)
    v = v + (f64(v_first) - v) * sigmoid(f64(v0) + f64(xv_v1) @ f64(v2))
    return v

@@ -1,0 +1,344 @@
+from contextlib import ExitStack
+
+import concourse.mybir as mybir
+from concourse.masks import make_identity
+
+F32 = mybir.dt.float32
+BF16 = mybir.dt.bfloat16
+I32 = mybir.dt.int32
+U8 = mybir.dt.uint8
+U32 = mybir.dt.uint32
+FP8X4 = mybir.dt.float8_e4m3fn_x4
+FP4X4 = mybir.dt.float4_e2m1fn_x4
+ALU = mybir.AluOpType
+ACT = mybir.ActivationFunctionType
+
+P = 128
+TOKENS = 4096
+SEQ = 1024
+C = 1024
+PACK = 4
+K_PASS = P * PACK
+PASSES = C // K_PASS
+CHUNK = 512
+N_CHUNKS = TOKENS // CHUNK
+TILES = CHUNK // P
+HALF = 512
+HALVES = C // HALF
+N_UNITS = TOKENS // P * HALVES
+UNITS = TILES * HALVES
+BLOCKS = C // P
+SCALE_JOBS = 2 * PASSES
+
+X_LEAD = 14
+GATE_LEAD = 10
+
+FLOPS = 2 * TOKENS * C * C + 2 * TOKENS * P * C
+
+
+def tile_full_tmix_params_pb_t_kernel(
+    tc, x, v_first, x_v, Wv_words, Wv_scales, v0, xv_v1, v2, out
+):
+    nc = tc.nc
+    x_rows = x.flatten_outer_dims()
+    vf_rows = v_first.flatten_outer_dims()
+    low_rows = xv_v1.flatten_outer_dims()
+    out_rows = out.flatten_outer_dims()
+
+    with ExitStack() as stack:
+        consts = stack.enter_context(tc.tile_pool(name="consts", bufs=1))
+        x_pool = stack.enter_context(tc.tile_pool(name="x", bufs=3))
+        vf_pool = stack.enter_context(tc.tile_pool(name="vf", bufs=2))
+        low_pool = stack.enter_context(tc.tile_pool(name="low", bufs=2))
+        own_pool = stack.enter_context(tc.tile_pool(name="own", bufs=3))
+        next_pool = stack.enter_context(tc.tile_pool(name="next", bufs=4))
+        xv_pool = stack.enter_context(tc.tile_pool(name="xv", bufs=1))
+        code_pool = stack.enter_context(tc.tile_pool(name="codes", bufs=2))
+        gate_pool = stack.enter_context(tc.tile_pool(name="gate", bufs=18))
+        diff_pool = stack.enter_context(tc.tile_pool(name="diff", bufs=4))
+        out_pool = stack.enter_context(tc.tile_pool(name="out", bufs=3))
+        psum_prep = stack.enter_context(tc.psum_pool(name="psum_prep", bufs=3))
+        psum_p = stack.enter_context(tc.psum_pool(name="psum_p", bufs=3))
+        psum_gate = stack.enter_context(tc.psum_pool(name="psum_gate", bufs=2))
+        stack.enter_context(tc.manual_schedule())
+
+        x_tiles = {}
+        low_tiles = {}
+        vf_tiles = {}
+
+        def load_x(chunk):
+            rows = slice(CHUNK * chunk, CHUNK * (chunk + 1))
+            x_sb = x_pool.tile([P, TILES, C], BF16)
+            nc.sync.dma_start(
+                out=x_sb[:], in_=x_rows[rows, :].rearrange("(j p) c -> p j c", p=P)
+            )
+            x_tiles[chunk] = x_sb
+            low_sb = low_pool.tile([P, TILES, P], BF16)
+            nc.sync.dma_start(
+                out=low_sb[:], in_=low_rows[rows, :].rearrange("(j p) d -> p j d", p=P)
+            )
+            low_tiles[chunk] = low_sb
+
+        def load_v_first(chunk):
+            rows = slice(CHUNK * chunk, CHUNK * (chunk + 1))
+            vf_sb = vf_pool.tile([P, TILES, C], BF16)
+            nc.sync.dma_start(
+                out=vf_sb[:], in_=vf_rows[rows, :].rearrange("(j p) c -> p j c", p=P)
+            )
+            vf_tiles[chunk] = vf_sb
+
+        mix_bf = consts.tile([P, PASSES, PACK], BF16)
+        nc.sync.dma_start(
+            out=mix_bf[:], in_=x_v.rearrange("(g p t) -> p g t", g=PASSES, p=P)
+        )
+        v0_rows = consts.tile([P, P], BF16)
+        nc.vector.memset(v0_rows[:], 0.0)
+        nc.sync.dma_start(
+            out=v0_rows[0:BLOCKS, :], in_=v0.rearrange("(r c) -> r c", c=P)
+        )
+        load_x(0)
+        v2_sb = consts.tile([P, C], BF16)
+        nc.sync.dma_start(out=v2_sb[:], in_=v2)
+        w_words = consts.tile([P, PASSES, 2 * C], U8, align_bytes=64)
+        w_scales = consts.tile([P, PASSES, C], U8, align_bytes=64)
+        nc.vector.memset(w_scales[:].bitcast(I32), 0)
+        for g in range(PASSES):
+            nc.sync.dma_start(
+                out=w_words[:, g, :].bitcast(I32), in_=Wv_words[g].bitcast(I32)
+            )
+        for g in range(PASSES):
+            for quad in range(4):
+                nc.sync.dma_start(
+                    out=w_scales[32 * quad : 32 * quad + 4, g, :].bitcast(I32),
+                    in_=Wv_scales[g, 4 * quad : 4 * quad + 4, :].bitcast(I32),
+                )
+
+        ident_f32 = consts.tile([P, P], F32)
+        make_identity(nc, ident_f32[:])
+        ident_bf = consts.tile([P, P], BF16)
+        make_identity(nc, ident_bf[:])
+
+        warm = consts.tile([P, 1], F32)
+        nc.vector.memset(warm[:], 0.0)
+        nc.scalar.activation(out=warm[:], in_=warm[:], func=ACT.Sigmoid)
+
+        mix = consts.tile([P, PASSES * PACK], F32)
+        nc.vector.tensor_copy(out=mix[:], in_=mix_bf[:].rearrange("p g t -> p (g t)"))
+        one_minus_mix = consts.tile([P, PASSES * PACK], F32)
+        nc.vector.tensor_scalar(
+            out=one_minus_mix[:],
+            in0=mix_bf[:].rearrange("p g t -> p (g t)"),
+            scalar1=-1.0,
+            scalar2=1.0,
+            op0=ALU.mult,
+            op1=ALU.add,
+        )
+
+        v0_ps = psum_prep.tile([P, P], BF16, tag="prep")
+        nc.tensor.transpose(v0_ps[:], v0_rows[:], ident_bf[:])
+        v0_cols = consts.tile([P, BLOCKS], F32)
+        nc.vector.tensor_copy(out=v0_cols[:], in_=v0_ps[:, 0:BLOCKS])
+
+        own_tiles = {}
+        next_tiles = {}
+        xv_tiles = {}
+        code_tiles = {}
+        scale_tiles = {}
+        low_t_tiles = {}
+        gate_t_tiles = {}
+        gate_banks = {}
+        p_banks = {}
+        diff_tiles = {}
+        out_tiles = {}
+
+        def scale_x(job):
+            chunk, g, u = job // SCALE_JOBS, (job % SCALE_JOBS) // 2, job % 2
+            if u == 0:
+                own = own_pool.tile([P, PACK, CHUNK], F32)
+                own_tiles[(chunk, g)] = own
+                nxt = next_pool.tile([P, PACK, CHUNK], F32)
+                next_tiles[(chunk, g)] = nxt
+            own = own_tiles[(chunk, g)]
+            nxt = next_tiles[(chunk, g)]
+            x_t = psum_prep.tile([P, CHUNK], F32, tag="prep")
+            for j in range(TILES):
+                words = x_tiles[chunk][:, j, :].bitcast(F32)
+                nc.tensor.transpose(
+                    x_t[:, P * j : P * (j + 1)],
+                    words[:, 256 * g + u : 256 * (g + 1) : 2],
+                    ident_f32[:],
+                )
+            pairs = x_t[:].bitcast(BF16).rearrange("p (r e) -> p r e", e=2)
+            for e in range(2):
+                t = 2 * u + e
+                col = PACK * g + t
+                nc.scalar.activation(
+                    out=own[:, t, :],
+                    in_=pairs[:, :, e],
+                    func=ACT.Copy,
+                    scale=one_minus_mix[:, col : col + 1],
+                )
+                nc.scalar.activation(
+                    out=nxt[:, t, :],
+                    in_=pairs[:, :, e],
+                    func=ACT.Copy,
+                    scale=mix[:, col : col + 1],
+                )
+
+        def mix_tokens(chunk, g):
+            if g == 0:
+                xv = xv_pool.tile([P, PASSES, CHUNK, PACK], BF16, align_bytes=64)
+                xv_tiles[chunk] = xv
+            xv = xv_tiles[chunk]
+            own = own_tiles[(chunk, g)]
+            nxt = next_tiles[(chunk, g)]
+            if (CHUNK * chunk) % SEQ == 0:
+                nc.gpsimd.tensor_copy(out=xv[:, g, 0, :], in_=own[:, :, 0])
+            else:
+                nc.gpsimd.tensor_tensor(
+                    out=xv[:, g, 0, :],
+                    in0=own[:, :, 0],
+                    in1=next_tiles[(chunk - 1, g)][:, :, CHUNK - 1],
+                    op=ALU.add,
+                )
+            nc.gpsimd.tensor_tensor(
+                out=xv[:, g, 1:CHUNK, :],
+                in0=own[:, :, 1:CHUNK].rearrange("p t r -> p r t"),
+                in1=nxt[:, :, 0 : CHUNK - 1].rearrange("p t r -> p r t"),
+                op=ALU.add,
+            )
+
+        def quantise(chunk):
+            codes = code_pool.tile([P, PASSES, CHUNK], U32, align_bytes=64)
+            scales = code_pool.tile([P, PASSES, CHUNK], U8, align_bytes=64)
+            nc.vector.quantize_mx(
+                out=codes[:].rearrange("p g r -> p (g r)").bitcast(FP8X4),
+                scales=scales[:].rearrange("p g r -> p (g r)"),
+                in_=xv_tiles[chunk][:].rearrange("p g r t -> p (g r t)"),
+            )
+            code_tiles[chunk] = codes
+            scale_tiles[chunk] = scales
+
+        def turn_low_rank(chunk):
+            low_ps = psum_prep.tile([P, CHUNK], BF16, tag="prep")
+            for j in range(TILES):
+                nc.tensor.transpose(
+                    low_ps[:, P * j : P * (j + 1)], low_tiles[chunk][:, j, :], ident_bf[:]
+                )
+            low_t = low_pool.tile([P, CHUNK], BF16)
+            nc.scalar.copy(out=low_t[:], in_=low_ps[:])
+            low_t_tiles[chunk] = low_t
+
+        def gate_block(job):
+            chunk, b = job // BLOCKS, job % BLOCKS
+            z_t = psum_prep.tile([P, CHUNK], F32, tag="prep")
+            nc.tensor.matmul(
+                out=z_t[:],
+                lhsT=v2_sb[:, P * b : P * (b + 1)],
+                rhs=low_t_tiles[chunk][:],
+                start=True,
+                stop=True,
+            )
+            gate_t = gate_pool.tile([P, CHUNK], F32)
+            nc.scalar.activation(
+                out=gate_t[:],
+                in_=z_t[:],
+                func=ACT.Sigmoid,
+                bias=v0_cols[:, b : b + 1],
+                scale=1.0,
+            )
+            gate_t_tiles[(chunk, b)] = gate_t
+
+        def where(unit):
+            return unit // UNITS, (unit % UNITS) // HALVES, unit % HALVES
+
+        def turn_gate(unit):
+            chunk, j, h = where(unit)
+            gate = psum_gate.tile([P, HALF], F32)
+            for q in range(HALF // P):
+                nc.tensor.transpose(
+                    gate[:, P * q : P * (q + 1)],
+                    gate_t_tiles[(chunk, (HALF // P) * h + q)][:, P * j : P * (j + 1)],
+                    ident_f32[:],
+                )
+            gate_banks[unit] = gate
+
+        def project(unit):
+            chunk, j, h = where(unit)
+            p_ps = psum_p.tile([P, HALF], F32)
+            for g in range(PASSES):
+                nc.tensor.matmul_mx(
+                    out=p_ps[:],
+                    lhsT=code_tiles[chunk][:, g, P * j : P * (j + 1)].bitcast(FP8X4),
+                    lhsT_scale=scale_tiles[chunk][:, g, P * j : P * (j + 1)],
+                    rhs=w_words[:, g, 2 * HALF * h : 2 * HALF * (h + 1)].bitcast(FP4X4),
+                    rhs_scale=w_scales[:, g, HALF * h : HALF * (h + 1)],
+                    start=(g == 0),
+                    stop=(g == PASSES - 1),
+                )
+            p_banks[unit] = p_ps
+
+        def subtract(unit):
+            chunk, j, h = where(unit)
+            diff = diff_pool.tile([P, HALF], F32)
+            nc.vector.tensor_tensor(
+                out=diff[:],
+                in0=vf_tiles[chunk][:, j, HALF * h : HALF * (h + 1)],
+                in1=p_banks[unit][:],
+                op=ALU.subtract,
+            )
+            diff_tiles[unit] = diff
+
+        def apply_gate(unit):
+            diff = diff_tiles[unit]
+            nc.vector.tensor_tensor(
+                out=diff[:], in0=diff[:], in1=gate_banks[unit][:], op=ALU.mult
+            )
+
+        def add_back(unit):
+            h = unit % HALVES
+            token_tile = unit // HALVES
+            if h == 0:
+                result = out_pool.tile([P, C], F32)
+                out_tiles[token_tile] = result
+            result = out_tiles[token_tile]
+            nc.vector.tensor_tensor(
+                out=result[:, HALF * h : HALF * (h + 1)],
+                in0=diff_tiles[unit][:],
+                in1=p_banks[unit][:],
+                op=ALU.add,
+            )
+            if h == HALVES - 1:
+                nc.sync.dma_start(
+                    out=out_rows[P * token_tile : P * (token_tile + 1), :], in_=result[:]
+                )
+
+        for tick in range(-X_LEAD, N_UNITS + 2):
+            if 0 <= tick - 2 < N_UNITS:
+                add_back(tick - 2)
+            if 0 <= tick < N_UNITS:
+                subtract(tick)
+            if 0 <= tick - 1 < N_UNITS:
+                apply_gate(tick - 1)
+            if (tick + 2) % UNITS == 0 and 0 <= (tick + 2) // UNITS < N_CHUNKS:
+                quantise((tick + 2) // UNITS)
+
+            if (tick + X_LEAD) % UNITS == 0 and (tick + X_LEAD) // UNITS + 1 < N_CHUNKS:
+                load_x((tick + X_LEAD) // UNITS + 1)
+            if tick % UNITS == 0 and 0 <= tick // UNITS + 1 < N_CHUNKS:
+                load_v_first(tick // UNITS + 1)
+
+            gate_job = tick + GATE_LEAD
+            if 0 <= gate_job < N_CHUNKS * BLOCKS and gate_job % BLOCKS == 0:
+                turn_low_rank(gate_job // BLOCKS)
+            if (tick + X_LEAD) % 2 == 0 and (tick + X_LEAD) // 2 < N_CHUNKS * SCALE_JOBS:
+                scale_job = (tick + X_LEAD) // 2
+                scale_x(scale_job)
+                if scale_job % 2 == 1:
+                    mix_tokens(scale_job // SCALE_JOBS, (scale_job % SCALE_JOBS) // 2)
+            if 0 <= tick < N_UNITS:
+                turn_gate(tick)
+            if 0 <= tick + 1 < N_UNITS:
+                project(tick + 1)
+            if 0 <= gate_job < N_CHUNKS * BLOCKS:
+                gate_block(gate_job)

@@ -52,7 +52,7 @@ def tile_full_tmix_params_pb_t_kernel(
         low_pool = stack.enter_context(tc.tile_pool(name="low", bufs=2))
         own_pool = stack.enter_context(tc.tile_pool(name="own", bufs=3))
         next_pool = stack.enter_context(tc.tile_pool(name="next", bufs=4))
-        xv_pool = stack.enter_context(tc.tile_pool(name="xv", bufs=1))
+        xv_pool = stack.enter_context(tc.tile_pool(name="xv", bufs=2))
         code_pool = stack.enter_context(tc.tile_pool(name="codes", bufs=2))
         gate_pool = stack.enter_context(tc.tile_pool(name="gate", bufs=18))
         diff_pool = stack.enter_context(tc.tile_pool(name="diff", bufs=4))
@@ -193,15 +193,15 @@ def tile_full_tmix_params_pb_t_kernel(
             own = own_tiles[(chunk, g)]
             nxt = next_tiles[(chunk, g)]
             if (CHUNK * chunk) % SEQ == 0:
-                nc.gpsimd.tensor_copy(out=xv[:, g, 0, :], in_=own[:, :, 0])
+                nc.vector.tensor_copy(out=xv[:, g, 0, :], in_=own[:, :, 0])
             else:
-                nc.gpsimd.tensor_tensor(
+                nc.vector.tensor_tensor(
                     out=xv[:, g, 0, :],
                     in0=own[:, :, 0],
                     in1=next_tiles[(chunk - 1, g)][:, :, CHUNK - 1],
                     op=ALU.add,
                 )
-            nc.gpsimd.tensor_tensor(
+            nc.vector.tensor_tensor(
                 out=xv[:, g, 1:CHUNK, :],
                 in0=own[:, :, 1:CHUNK].rearrange("p t r -> p r t"),
                 in1=nxt[:, :, 0 : CHUNK - 1].rearrange("p t r -> p r t"),

@@ -31,7 +31,7 @@ BLOCKS = C // P
 SCALE_JOBS = 2 * PASSES
 
 X_LEAD = 14
-GATE_LEAD = 10
+GATE_LEAD = 8
 
 FLOPS = 2 * TOKENS * C * C + 2 * TOKENS * P * C
 
@@ -51,8 +51,7 @@ def tile_full_tmix_params_pb_t_kernel(
         vf_pool = stack.enter_context(tc.tile_pool(name="vf", bufs=2))
         low_pool = stack.enter_context(tc.tile_pool(name="low", bufs=2))
         own_pool = stack.enter_context(tc.tile_pool(name="own", bufs=3))
-        next_pool = stack.enter_context(tc.tile_pool(name="next", bufs=4))
-        xv_pool = stack.enter_context(tc.tile_pool(name="xv", bufs=2))
+        xv_pool = stack.enter_context(tc.tile_pool(name="xv", bufs=1))
         code_pool = stack.enter_context(tc.tile_pool(name="codes", bufs=2))
         gate_pool = stack.enter_context(tc.tile_pool(name="gate", bufs=18))
         diff_pool = stack.enter_context(tc.tile_pool(name="diff", bufs=4))
@@ -139,8 +138,18 @@ def tile_full_tmix_params_pb_t_kernel(
         v0_cols = consts.tile([P, BLOCKS], F32)
         nc.vector.tensor_copy(out=v0_cols[:], in_=v0_ps[:, 0:BLOCKS])
 
+        zeros = consts.tile([P, PACK], F32)
+        nc.vector.memset(zeros[:], 0.0)
+        before_tiles = {}
+        for parity in range(2):
+            for g in range(PASSES):
+                before = consts.tile(
+                    [P, PACK, SEQ + PACK], F32, name="before_%d_%d" % (parity, g)
+                )
+                nc.scalar.copy(out=before[:, :, 0], in_=zeros[:])
+                before_tiles[(parity, g)] = before
+
         own_tiles = {}
-        next_tiles = {}
         xv_tiles = {}
         code_tiles = {}
         scale_tiles = {}
@@ -151,15 +160,17 @@ def tile_full_tmix_params_pb_t_kernel(
         diff_tiles = {}
         out_tiles = {}
 
+        def before_of(chunk, g):
+            sequence, first = divmod(CHUNK * chunk, SEQ)
+            return before_tiles[(sequence % 2, g)], first
+
         def scale_x(job):
             chunk, g, u = job // SCALE_JOBS, (job % SCALE_JOBS) // 2, job % 2
             if u == 0:
                 own = own_pool.tile([P, PACK, CHUNK], F32)
                 own_tiles[(chunk, g)] = own
-                nxt = next_pool.tile([P, PACK, CHUNK], F32)
-                next_tiles[(chunk, g)] = nxt
             own = own_tiles[(chunk, g)]
-            nxt = next_tiles[(chunk, g)]
+            before, first = before_of(chunk, g)
             x_t = psum_prep.tile([P, CHUNK], F32, tag="prep")
             for j in range(TILES):
                 words = x_tiles[chunk][:, j, :].bitcast(F32)
@@ -179,7 +190,7 @@ def tile_full_tmix_params_pb_t_kernel(
                     scale=one_minus_mix[:, col : col + 1],
                 )
                 nc.scalar.activation(
-                    out=nxt[:, t, :],
+                    out=before[:, t, first + 1 : first + 1 + CHUNK],
                     in_=pairs[:, :, e],
                     func=ACT.Copy,
                     scale=mix[:, col : col + 1],
@@ -190,21 +201,13 @@ def tile_full_tmix_params_pb_t_kernel(
                 xv = xv_pool.tile([P, PASSES, CHUNK, PACK], BF16, align_bytes=64)
                 xv_tiles[chunk] = xv
             xv = xv_tiles[chunk]
-            own = own_tiles[(chunk, g)]
-            nxt = next_tiles[(chunk, g)]
-            if (CHUNK * chunk) % SEQ == 0:
-                nc.vector.tensor_copy(out=xv[:, g, 0, :], in_=own[:, :, 0])
-            else:
-                nc.vector.tensor_tensor(
-                    out=xv[:, g, 0, :],
-                    in0=own[:, :, 0],
-                    in1=next_tiles[(chunk - 1, g)][:, :, CHUNK - 1],
-                    op=ALU.add,
-                )
-            nc.vector.tensor_tensor(
-                out=xv[:, g, 1:CHUNK, :],
-                in0=own[:, :, 1:CHUNK].rearrange("p t r -> p r t"),
-                in1=nxt[:, :, 0 : CHUNK - 1].rearrange("p t r -> p r t"),
+            before, first = before_of(chunk, g)
+            nc.gpsimd.tensor_tensor(
+                out=xv[:, g, :, :].rearrange("p (c i) t -> p c t i", i=4),
+                in0=own_tiles[(chunk, g)][:].rearrange("p t (c i) -> p c t i", i=4),
+                in1=before[:, :, first : first + CHUNK].rearrange(
+                    "p t (c i) -> p c t i", i=4
+                ),
                 op=ALU.add,
             )
 
@@ -316,10 +319,10 @@ def tile_full_tmix_params_pb_t_kernel(
         for tick in range(-X_LEAD, N_UNITS + 2):
             if 0 <= tick - 2 < N_UNITS:
                 add_back(tick - 2)
-            if 0 <= tick < N_UNITS:
-                subtract(tick)
             if 0 <= tick - 1 < N_UNITS:
                 apply_gate(tick - 1)
+            if 0 <= tick < N_UNITS:
+                subtract(tick)
             if (tick + 2) % UNITS == 0 and 0 <= (tick + 2) // UNITS < N_CHUNKS:
                 quantise((tick + 2) // UNITS)
 

@@ -32,6 +32,8 @@ SCALE_JOBS = 2 * PASSES
 
 X_LEAD = 14
 GATE_LEAD = 8
+LOW_LEAD = GATE_LEAD + 2
+BACK_BANKS = 4
 
 FLOPS = 2 * TOKENS * C * C + 2 * TOKENS * P * C
 
@@ -55,10 +57,9 @@ def tile_full_tmix_params_pb_t_kernel(
         code_pool = stack.enter_context(tc.tile_pool(name="codes", bufs=2))
         gate_pool = stack.enter_context(tc.tile_pool(name="gate", bufs=18))
         diff_pool = stack.enter_context(tc.tile_pool(name="diff", bufs=4))
-        out_pool = stack.enter_context(tc.tile_pool(name="out", bufs=3))
-        psum_prep = stack.enter_context(tc.psum_pool(name="psum_prep", bufs=3))
-        psum_p = stack.enter_context(tc.psum_pool(name="psum_p", bufs=3))
-        psum_gate = stack.enter_context(tc.psum_pool(name="psum_gate", bufs=2))
+        out_pool = stack.enter_context(tc.tile_pool(name="out", bufs=6))
+        psum_prep = stack.enter_context(tc.psum_pool(name="psum_prep", bufs=4))
+        psum_back = stack.enter_context(tc.psum_pool(name="psum_back", bufs=1))
         stack.enter_context(tc.manual_schedule())
 
         x_tiles = {}
@@ -68,9 +69,12 @@ def tile_full_tmix_params_pb_t_kernel(
         def load_x(chunk):
             rows = slice(CHUNK * chunk, CHUNK * (chunk + 1))
             x_sb = x_pool.tile([P, TILES, C], BF16)
-            nc.sync.dma_start(
-                out=x_sb[:], in_=x_rows[rows, :].rearrange("(j p) c -> p j c", p=P)
-            )
+            for g in range(PASSES):
+                channels = slice(K_PASS * g, K_PASS * (g + 1))
+                nc.sync.dma_start(
+                    out=x_sb[:, :, channels],
+                    in_=x_rows[rows, channels].rearrange("(j p) c -> p j c", p=P),
+                )
             x_tiles[chunk] = x_sb
             low_sb = low_pool.tile([P, TILES, P], BF16)
             nc.sync.dma_start(
@@ -158,13 +162,12 @@ def tile_full_tmix_params_pb_t_kernel(
         gate_banks = {}
         p_banks = {}
         diff_tiles = {}
-        out_tiles = {}
 
         def before_of(chunk, g):
             sequence, first = divmod(CHUNK * chunk, SEQ)
             return before_tiles[(sequence % 2, g)], first
 
-        def scale_x(job):
+        def scale_x(job, vector_helps):
             chunk, g, u = job // SCALE_JOBS, (job % SCALE_JOBS) // 2, job % 2
             if u == 0:
                 own = own_pool.tile([P, PACK, CHUNK], F32)
@@ -184,17 +187,27 @@ def tile_full_tmix_params_pb_t_kernel(
                 t = 2 * u + e
                 col = PACK * g + t
                 nc.scalar.activation(
-                    out=own[:, t, :],
-                    in_=pairs[:, :, e],
-                    func=ACT.Copy,
-                    scale=one_minus_mix[:, col : col + 1],
-                )
-                nc.scalar.activation(
                     out=before[:, t, first + 1 : first + 1 + CHUNK],
                     in_=pairs[:, :, e],
                     func=ACT.Copy,
                     scale=mix[:, col : col + 1],
                 )
+            for e in range(2):
+                t = 2 * u + e
+                col = PACK * g + t
+                if vector_helps:
+                    nc.vector.tensor_scalar_mul(
+                        out=own[:, t, :],
+                        in0=pairs[:, :, e],
+                        scalar1=one_minus_mix[:, col : col + 1],
+                    )
+                else:
+                    nc.scalar.activation(
+                        out=own[:, t, :],
+                        in_=pairs[:, :, e],
+                        func=ACT.Copy,
+                        scale=one_minus_mix[:, col : col + 1],
+                    )
 
         def mix_tokens(chunk, g):
             if g == 0:
@@ -257,7 +270,7 @@ def tile_full_tmix_params_pb_t_kernel(
 
         def turn_gate(unit):
             chunk, j, h = where(unit)
-            gate = psum_gate.tile([P, HALF], F32)
+            gate = psum_back.tile([P, HALF], F32, tag="back%d" % ((unit + 2) % BACK_BANKS))
             for q in range(HALF // P):
                 nc.tensor.transpose(
                     gate[:, P * q : P * (q + 1)],
@@ -268,7 +281,7 @@ def tile_full_tmix_params_pb_t_kernel(
 
         def project(unit):
             chunk, j, h = where(unit)
-            p_ps = psum_p.tile([P, HALF], F32)
+            p_ps = psum_back.tile([P, HALF], F32, tag="back%d" % (unit % BACK_BANKS))
             for g in range(PASSES):
                 nc.tensor.matmul_mx(
                     out=p_ps[:],
@@ -301,20 +314,16 @@ def tile_full_tmix_params_pb_t_kernel(
         def add_back(unit):
             h = unit % HALVES
             token_tile = unit // HALVES
-            if h == 0:
-                result = out_pool.tile([P, C], F32)
-                out_tiles[token_tile] = result
-            result = out_tiles[token_tile]
+            result = out_pool.tile([P, HALF], F32)
             nc.vector.tensor_tensor(
-                out=result[:, HALF * h : HALF * (h + 1)],
-                in0=diff_tiles[unit][:],
-                in1=p_banks[unit][:],
-                op=ALU.add,
+                out=result[:], in0=diff_tiles[unit][:], in1=p_banks[unit][:], op=ALU.add
             )
-            if h == HALVES - 1:
-                nc.sync.dma_start(
-                    out=out_rows[P * token_tile : P * (token_tile + 1), :], in_=result[:]
-                )
+            nc.sync.dma_start(
+                out=out_rows[
+                    P * token_tile : P * (token_tile + 1), HALF * h : HALF * (h + 1)
+                ],
+                in_=result[:],
+            )
 
         for tick in range(-X_LEAD, N_UNITS + 2):
             if 0 <= tick - 2 < N_UNITS:
@@ -332,11 +341,11 @@ def tile_full_tmix_params_pb_t_kernel(
                 load_v_first(tick // UNITS + 1)
 
             gate_job = tick + GATE_LEAD
-            if 0 <= gate_job < N_CHUNKS * BLOCKS and gate_job % BLOCKS == 0:
-                turn_low_rank(gate_job // BLOCKS)
+            if (tick + LOW_LEAD) % UNITS == 0 and 0 <= (tick + LOW_LEAD) // UNITS < N_CHUNKS:
+                turn_low_rank((tick + LOW_LEAD) // UNITS)
             if (tick + X_LEAD) % 2 == 0 and (tick + X_LEAD) // 2 < N_CHUNKS * SCALE_JOBS:
                 scale_job = (tick + X_LEAD) // 2
-                scale_x(scale_job)
+                scale_x(scale_job, vector_helps=(tick < 0))
                 if scale_job % 2 == 1:
                     mix_tokens(scale_job // SCALE_JOBS, (scale_job % SCALE_JOBS) // 2)
             if 0 <= tick < N_UNITS:

@@ -215,7 +215,8 @@ def tile_full_tmix_params_pb_t_kernel(
                 xv_tiles[chunk] = xv
             xv = xv_tiles[chunk]
             before, first = before_of(chunk, g)
-            nc.gpsimd.tensor_tensor(
+            engine = nc.vector if (chunk == 0 and g == PASSES - 1) else nc.gpsimd
+            engine.tensor_tensor(
                 out=xv[:, g, :, :].rearrange("p (c i) t -> p c t i", i=4),
                 in0=own_tiles[(chunk, g)][:].rearrange("p t (c i) -> p c t i", i=4),
                 in1=before[:, :, first : first + CHUNK].rearrange(

@@ -30,10 +30,19 @@ UNITS = TILES * HALVES
 BLOCKS = C // P
 SCALE_JOBS = 2 * PASSES
 
-X_LEAD = 14
-GATE_LEAD = 8
-LOW_LEAD = GATE_LEAD + 2
+N_STEPS = TOKENS // P
+X_LEAD = 7
+GATE_LEAD = 5
+LOW_LEAD = GATE_LEAD + 1
+QUANT_LEAD = 1
 BACK_BANKS = 4
+POOL_TILES = 2
+ALL_POOL_FROM = 27
+ALL_POOL_TO = 30
+HEAD_HELP = (2, 2, 2, 2, 2, 2, 2, 2)
+VECTOR_JOBS = ()
+CHUNK_STORE_LAG = 3
+TILE_STORE_LAG = 1
 
 FLOPS = 2 * TOKENS * C * C + 2 * TOKENS * P * C
 
@@ -49,15 +58,16 @@ def tile_full_tmix_params_pb_t_kernel(
 
     with ExitStack() as stack:
         consts = stack.enter_context(tc.tile_pool(name="consts", bufs=1))
-        x_pool = stack.enter_context(tc.tile_pool(name="x", bufs=3))
-        vf_pool = stack.enter_context(tc.tile_pool(name="vf", bufs=2))
+        x_pool = stack.enter_context(tc.tile_pool(name="x", bufs=2))
+        vf_pool = stack.enter_context(tc.tile_pool(name="vf", bufs=3))
         low_pool = stack.enter_context(tc.tile_pool(name="low", bufs=2))
         own_pool = stack.enter_context(tc.tile_pool(name="own", bufs=3))
         xv_pool = stack.enter_context(tc.tile_pool(name="xv", bufs=1))
         code_pool = stack.enter_context(tc.tile_pool(name="codes", bufs=2))
-        gate_pool = stack.enter_context(tc.tile_pool(name="gate", bufs=18))
+        gate_pool = stack.enter_context(tc.tile_pool(name="gate", bufs=16))
         diff_pool = stack.enter_context(tc.tile_pool(name="diff", bufs=4))
-        out_pool = stack.enter_context(tc.tile_pool(name="out", bufs=6))
+        kept_pool = stack.enter_context(tc.tile_pool(name="kept", bufs=4))
+        out_pool = stack.enter_context(tc.tile_pool(name="out", bufs=5))
         psum_prep = stack.enter_context(tc.psum_pool(name="psum_prep", bufs=4))
         psum_back = stack.enter_context(tc.psum_pool(name="psum_back", bufs=1))
         stack.enter_context(tc.manual_schedule())
@@ -139,8 +149,10 @@ def tile_full_tmix_params_pb_t_kernel(
 
         v0_ps = psum_prep.tile([P, P], BF16, tag="prep")
         nc.tensor.transpose(v0_ps[:], v0_rows[:], ident_bf[:])
-        v0_cols = consts.tile([P, BLOCKS], F32)
-        nc.vector.tensor_copy(out=v0_cols[:], in_=v0_ps[:, 0:BLOCKS])
+        neg_v0_cols = consts.tile([P, BLOCKS], F32)
+        nc.vector.tensor_scalar_mul(
+            out=neg_v0_cols[:], in0=v0_ps[:, 0:BLOCKS], scalar1=-1.0
+        )
 
         zeros = consts.tile([P, PACK], F32)
         nc.vector.memset(zeros[:], 0.0)
@@ -162,12 +174,37 @@ def tile_full_tmix_params_pb_t_kernel(
         gate_banks = {}
         p_banks = {}
         diff_tiles = {}
+        kept_tiles = {}
+        bank_numbers = {}
+        free_banks = list(range(BACK_BANKS))
+        pending_stores = []
+
+        def take_bank():
+            bank = free_banks[0]
+            free_banks.remove(bank)
+            return bank
+
+        def where(unit):
+            return unit // UNITS, (unit % UNITS) // HALVES, unit % HALVES
+
+        def whole_tile_on_gpsimd(step):
+            return ALL_POOL_FROM <= step < ALL_POOL_TO
+
+        def on_gpsimd(unit):
+            chunk, j, h = where(unit)
+            return whole_tile_on_gpsimd(unit // HALVES) or (h == 1 and j < POOL_TILES)
+
+        def group_of(unit):
+            chunk, j, h = where(unit)
+            if whole_tile_on_gpsimd(unit // HALVES):
+                return ("tile", unit // HALVES), h
+            return ("chunk", chunk), j
 
         def before_of(chunk, g):
             sequence, first = divmod(CHUNK * chunk, SEQ)
             return before_tiles[(sequence % 2, g)], first
 
-        def scale_x(job, vector_helps):
+        def scale_x(job, on_vector):
             chunk, g, u = job // SCALE_JOBS, (job % SCALE_JOBS) // 2, job % 2
             if u == 0:
                 own = own_pool.tile([P, PACK, CHUNK], F32)
@@ -195,7 +232,7 @@ def tile_full_tmix_params_pb_t_kernel(
             for e in range(2):
                 t = 2 * u + e
                 col = PACK * g + t
-                if vector_helps:
+                if e >= 2 - on_vector:
                     nc.vector.tensor_scalar_mul(
                         out=own[:, t, :],
                         in0=pairs[:, :, e],
@@ -261,17 +298,14 @@ def tile_full_tmix_params_pb_t_kernel(
                 out=gate_t[:],
                 in_=z_t[:],
                 func=ACT.Sigmoid,
-                bias=v0_cols[:, b : b + 1],
-                scale=1.0,
+                bias=neg_v0_cols[:, b : b + 1],
+                scale=-1.0,
             )
             gate_t_tiles[(chunk, b)] = gate_t
 
-        def where(unit):
-            return unit // UNITS, (unit % UNITS) // HALVES, unit % HALVES
-
         def turn_gate(unit):
             chunk, j, h = where(unit)
-            gate = psum_back.tile([P, HALF], F32, tag="back%d" % ((unit + 2) % BACK_BANKS))
+            gate = psum_back.tile([P, HALF], F32, tag="back%d" % take_bank())
             for q in range(HALF // P):
                 nc.tensor.transpose(
                     gate[:, P * q : P * (q + 1)],
@@ -282,7 +316,7 @@ def tile_full_tmix_params_pb_t_kernel(
 
         def project(unit):
             chunk, j, h = where(unit)
-            p_ps = psum_back.tile([P, HALF], F32, tag="back%d" % (unit % BACK_BANKS))
+            p_ps = psum_back.tile([P, HALF], F32, tag="back%d" % take_bank())
             for g in range(PASSES):
                 nc.tensor.matmul_mx(
                     out=p_ps[:],
@@ -297,27 +331,48 @@ def tile_full_tmix_params_pb_t_kernel(
 
         def subtract(unit):
             chunk, j, h = where(unit)
-            diff = diff_pool.tile([P, HALF], F32)
+            if on_gpsimd(unit):
+                group, place = group_of(unit)
+                if group not in kept_tiles:
+                    if group[0] == "tile" and group[1] % 2 == 1:
+                        own = own_pool.tile([P, 2, HALF], F32)
+                        kept_tiles[group] = own
+                    else:
+                        kept = kept_pool.tile([P, 2, HALF], F32)
+                        kept_tiles[group] = kept
+                diff_tiles[unit] = kept_tiles[group][:, place, :]
+            else:
+                diff = diff_pool.tile([P, HALF], F32)
+                diff_tiles[unit] = diff[:]
             nc.vector.tensor_tensor(
-                out=diff[:],
+                out=diff_tiles[unit],
                 in0=vf_tiles[chunk][:, j, HALF * h : HALF * (h + 1)],
                 in1=p_banks[unit][:],
                 op=ALU.subtract,
             )
-            diff_tiles[unit] = diff
 
         def apply_gate(unit):
             diff = diff_tiles[unit]
-            nc.vector.tensor_tensor(
-                out=diff[:], in0=diff[:], in1=gate_banks[unit][:], op=ALU.mult
-            )
+            if on_gpsimd(unit):
+                nc.vector.tensor_tensor(
+                    out=diff, in0=diff, in1=gate_banks[unit][:], op=ALU.mult
+                )
+            else:
+                nc.vector.scalar_tensor_tensor(
+                    out=diff,
+                    in0=gate_banks[unit][:],
+                    scalar=1.0,
+                    in1=diff,
+                    op0=ALU.subtract,
+                    op1=ALU.mult,
+                )
 
         def add_back(unit):
             h = unit % HALVES
             token_tile = unit // HALVES
             result = out_pool.tile([P, HALF], F32)
             nc.vector.tensor_tensor(
-                out=result[:], in0=diff_tiles[unit][:], in1=p_banks[unit][:], op=ALU.add
+                out=result[:], in0=p_banks[unit][:], in1=diff_tiles[unit], op=ALU.subtract
             )
             nc.sync.dma_start(
                 out=out_rows[
@@ -326,32 +381,89 @@ def tile_full_tmix_params_pb_t_kernel(
                 in_=result[:],
             )
 
-        for tick in range(-X_LEAD, N_UNITS + 2):
-            if 0 <= tick - 2 < N_UNITS:
-                add_back(tick - 2)
-            if 0 <= tick - 1 < N_UNITS:
-                apply_gate(tick - 1)
-            if 0 <= tick < N_UNITS:
-                subtract(tick)
-            if (tick + 2) % UNITS == 0 and 0 <= (tick + 2) // UNITS < N_CHUNKS:
-                quantise((tick + 2) // UNITS)
+        def take_away(group, due):
+            kept = kept_tiles[group]
+            kind, number = group
+            if kind == "chunk":
+                vf_view = vf_tiles[number][:, 0:POOL_TILES, HALF : 2 * HALF]
+                rows = slice(CHUNK * number, CHUNK * number + P * POOL_TILES)
+                out_view = out_rows[rows, HALF : 2 * HALF].rearrange("(j p) c -> p j c", p=P)
+                kept_view = kept[:, 0:POOL_TILES, :]
+            else:
+                vf_view = vf_tiles[number // TILES][:, number % TILES, :].rearrange(
+                    "p (h c) -> p h c", h=HALVES
+                )
+                out_view = out_rows[P * number : P * (number + 1), :].rearrange(
+                    "p (h c) -> p h c", h=HALVES
+                )
+                kept_view = kept[:]
+            nc.gpsimd.tensor_tensor(out=kept_view, in0=vf_view, in1=kept_view, op=ALU.subtract)
+            pending_stores.extend([(due, out_view, kept_view)])
 
-            if (tick + X_LEAD) % UNITS == 0 and (tick + X_LEAD) // UNITS + 1 < N_CHUNKS:
-                load_x((tick + X_LEAD) // UNITS + 1)
-            if tick % UNITS == 0 and 0 <= tick // UNITS + 1 < N_CHUNKS:
-                load_v_first(tick // UNITS + 1)
+        def blend(step):
+            low_unit, high_unit = HALVES * step, HALVES * step + 1
+            banks = bank_numbers[step]
+            subtract(low_unit)
+            subtract(high_unit)
+            apply_gate(low_unit)
+            apply_gate(high_unit)
+            for unit, bank in ((low_unit, banks[0]), (high_unit, banks[1])):
+                if on_gpsimd(unit):
+                    free_banks.extend([bank])
+            free_banks.extend(banks[2:4])
+            for unit, bank in ((low_unit, banks[0]), (high_unit, banks[1])):
+                if not on_gpsimd(unit):
+                    add_back(unit)
+                    free_banks.extend([bank])
 
-            gate_job = tick + GATE_LEAD
-            if (tick + LOW_LEAD) % UNITS == 0 and 0 <= (tick + LOW_LEAD) // UNITS < N_CHUNKS:
-                turn_low_rank((tick + LOW_LEAD) // UNITS)
-            if (tick + X_LEAD) % 2 == 0 and (tick + X_LEAD) // 2 < N_CHUNKS * SCALE_JOBS:
-                scale_job = (tick + X_LEAD) // 2
-                scale_x(scale_job, vector_helps=(tick < 0))
-                if scale_job % 2 == 1:
-                    mix_tokens(scale_job // SCALE_JOBS, (scale_job % SCALE_JOBS) // 2)
-            if 0 <= tick < N_UNITS:
-                turn_gate(tick)
-            if 0 <= tick + 1 < N_UNITS:
-                project(tick + 1)
-            if 0 <= gate_job < N_CHUNKS * BLOCKS:
-                gate_block(gate_job)
+        for step in range(-X_LEAD, N_STEPS + max(CHUNK_STORE_LAG, TILE_STORE_LAG) + 1):
+            quant_chunk, at_chunk_start = divmod(step + QUANT_LEAD, TILES)
+            if at_chunk_start == 0 and 1 <= quant_chunk < N_CHUNKS:
+                quantise(quant_chunk)
+                if quant_chunk + 1 < N_CHUNKS:
+                    mix_tokens(quant_chunk + 1, 0)
+                    if ("chunk", quant_chunk - 1) in kept_tiles:
+                        take_away(("chunk", quant_chunk - 1), step + CHUNK_STORE_LAG)
+            if 0 <= step < N_STEPS:
+                blend(step)
+                if whole_tile_on_gpsimd(step):
+                    take_away(("tile", step), step + TILE_STORE_LAG)
+                    if step == ALL_POOL_FROM:
+                        for late_chunk in (N_CHUNKS - 2, N_CHUNKS - 1):
+                            if ("chunk", late_chunk) in kept_tiles:
+                                take_away(("chunk", late_chunk), step + TILE_STORE_LAG)
+
+            for due, out_view, kept_view in pending_stores:
+                if due == step:
+                    nc.sync.dma_start(out=out_view, in_=kept_view)
+            if (step + X_LEAD) % TILES == 0 and (step + X_LEAD) // TILES + 1 < N_CHUNKS:
+                load_x((step + X_LEAD) // TILES + 1)
+            if step % TILES == 0 and 0 <= step // TILES + 1 < N_CHUNKS:
+                load_v_first(step // TILES + 1)
+
+            if (step + LOW_LEAD) % TILES == 0 and 0 <= (step + LOW_LEAD) // TILES < N_CHUNKS:
+                turn_low_rank((step + LOW_LEAD) // TILES)
+            scale_job = step + X_LEAD
+            if scale_job < N_CHUNKS * SCALE_JOBS:
+                if step < 0:
+                    on_vector = HEAD_HELP[scale_job]
+                else:
+                    on_vector = 1 if scale_job % SCALE_JOBS in VECTOR_JOBS else 0
+                scale_x(scale_job, on_vector)
+                job_chunk, job_in_chunk = divmod(scale_job, SCALE_JOBS)
+                if job_chunk <= 1 and job_in_chunk == 1:
+                    mix_tokens(job_chunk, 0)
+                if job_in_chunk == SCALE_JOBS - 1:
+                    mix_tokens(job_chunk, 1)
+                    if job_chunk == 0:
+                        quantise(0)
+            for k in range(2):
+                gate_job = 2 * (step + GATE_LEAD) + k
+                if 0 <= gate_job < N_CHUNKS * BLOCKS:
+                    gate_block(gate_job)
+            if 0 <= step + 1 < N_STEPS:
+                bank_numbers[step + 1] = list(free_banks[0:BACK_BANKS])
+                project(HALVES * (step + 1))
+                project(HALVES * (step + 1) + 1)
+                turn_gate(HALVES * (step + 1))
+                turn_gate(HALVES * (step + 1) + 1)

@@ -41,6 +41,8 @@ ALL_POOL_FROM = 27
 ALL_POOL_TO = 30
 HEAD_HELP = (2, 2, 2, 2, 2, 2, 2, 2)
 VECTOR_JOBS = ()
+FIRST_SUM_AFTER = 4
+PE_ORDER = "XMPG"
 CHUNK_STORE_LAG = 3
 TILE_STORE_LAG = 1
 
@@ -192,7 +194,9 @@ def tile_full_tmix_params_pb_t_kernel(
 
         def on_gpsimd(unit):
             chunk, j, h = where(unit)
-            return whole_tile_on_gpsimd(unit // HALVES) or (h == 1 and j < POOL_TILES)
+            if unit // HALVES >= ALL_POOL_FROM:
+                return whole_tile_on_gpsimd(unit // HALVES)
+            return h == 1 and j < POOL_TILES
 
         def group_of(unit):
             chunk, j, h = where(unit)
@@ -220,30 +224,23 @@ def tile_full_tmix_params_pb_t_kernel(
                     ident_f32[:],
                 )
             pairs = x_t[:].bitcast(BF16).rearrange("p (r e) -> p r e", e=2)
+            scalings = []
             for e in range(2):
                 t = 2 * u + e
                 col = PACK * g + t
-                nc.scalar.activation(
-                    out=before[:, t, first + 1 : first + 1 + CHUNK],
-                    in_=pairs[:, :, e],
-                    func=ACT.Copy,
-                    scale=mix[:, col : col + 1],
+                scalings.extend(
+                    [(before[:, t, first + 1 : first + 1 + CHUNK], e, mix[:, col : col + 1])]
                 )
             for e in range(2):
                 t = 2 * u + e
                 col = PACK * g + t
-                if e >= 2 - on_vector:
-                    nc.vector.tensor_scalar_mul(
-                        out=own[:, t, :],
-                        in0=pairs[:, :, e],
-                        scalar1=one_minus_mix[:, col : col + 1],
-                    )
+                scalings.extend([(own[:, t, :], e, one_minus_mix[:, col : col + 1])])
+            for number, (target, e, factor) in enumerate(scalings):
+                if number >= len(scalings) - on_vector:
+                    nc.vector.tensor_scalar_mul(out=target, in0=pairs[:, :, e], scalar1=factor)
                 else:
                     nc.scalar.activation(
-                        out=own[:, t, :],
-                        in_=pairs[:, :, e],
-                        func=ACT.Copy,
-                        scale=one_minus_mix[:, col : col + 1],
+                        out=target, in_=pairs[:, :, e], func=ACT.Copy, scale=factor
                     )
 
         def mix_tokens(chunk, g):
@@ -338,7 +335,7 @@ def tile_full_tmix_params_pb_t_kernel(
                         own = own_pool.tile([P, 2, HALF], F32)
                         kept_tiles[group] = own
                     else:
-                        kept = kept_pool.tile([P, 2, HALF], F32)
+                        kept = kept_pool.tile([P, max(POOL_TILES, HALVES), HALF], F32)
                         kept_tiles[group] = kept
                 diff_tiles[unit] = kept_tiles[group][:, place, :]
             else:
@@ -396,7 +393,7 @@ def tile_full_tmix_params_pb_t_kernel(
                 out_view = out_rows[P * number : P * (number + 1), :].rearrange(
                     "p (h c) -> p h c", h=HALVES
                 )
-                kept_view = kept[:]
+                kept_view = kept[:, 0:HALVES, :]
             nc.gpsimd.tensor_tensor(out=kept_view, in0=vf_view, in1=kept_view, op=ALU.subtract)
             pending_stores.extend([(due, out_view, kept_view)])
 
@@ -441,29 +438,34 @@ def tile_full_tmix_params_pb_t_kernel(
             if step % TILES == 0 and 0 <= step // TILES + 1 < N_CHUNKS:
                 load_v_first(step // TILES + 1)
 
-            if (step + LOW_LEAD) % TILES == 0 and 0 <= (step + LOW_LEAD) // TILES < N_CHUNKS:
-                turn_low_rank((step + LOW_LEAD) // TILES)
-            scale_job = step + X_LEAD
-            if scale_job < N_CHUNKS * SCALE_JOBS:
-                if step < 0:
-                    on_vector = HEAD_HELP[scale_job]
-                else:
-                    on_vector = 1 if scale_job % SCALE_JOBS in VECTOR_JOBS else 0
-                scale_x(scale_job, on_vector)
-                job_chunk, job_in_chunk = divmod(scale_job, SCALE_JOBS)
-                if job_chunk <= 1 and job_in_chunk == 1:
-                    mix_tokens(job_chunk, 0)
-                if job_in_chunk == SCALE_JOBS - 1:
-                    mix_tokens(job_chunk, 1)
-                    if job_chunk == 0:
-                        quantise(0)
-            for k in range(2):
-                gate_job = 2 * (step + GATE_LEAD) + k
-                if 0 <= gate_job < N_CHUNKS * BLOCKS:
-                    gate_block(gate_job)
-            if 0 <= step + 1 < N_STEPS:
-                bank_numbers[step + 1] = list(free_banks[0:BACK_BANKS])
-                project(HALVES * (step + 1))
-                project(HALVES * (step + 1) + 1)
-                turn_gate(HALVES * (step + 1))
-                turn_gate(HALVES * (step + 1) + 1)
+            for part in PE_ORDER:
+                if part == "X":
+                    scale_job = step + X_LEAD
+                    if scale_job < N_CHUNKS * SCALE_JOBS:
+                        if step < 0:
+                            on_vector = HEAD_HELP[scale_job]
+                        else:
+                            on_vector = 1 if scale_job % SCALE_JOBS in VECTOR_JOBS else 0
+                        scale_x(scale_job, on_vector)
+                        job_chunk, job_in_chunk = divmod(scale_job, SCALE_JOBS)
+                        if job_chunk <= 1 and job_in_chunk == 1:
+                            mix_tokens(job_chunk, 0)
+                        if job_in_chunk == SCALE_JOBS - 1 and job_chunk > 0:
+                            mix_tokens(job_chunk, 1)
+                        if scale_job == FIRST_SUM_AFTER:
+                            mix_tokens(0, 1)
+                            quantise(0)
+                    if (step + LOW_LEAD) % TILES == 0 and 0 <= (step + LOW_LEAD) // TILES < N_CHUNKS:
+                        turn_low_rank((step + LOW_LEAD) // TILES)
+                if part in ("M", "m", "n"):
+                    for k in range(2):
+                        gate_job = 2 * (step + GATE_LEAD) + k
+                        if 0 <= gate_job < N_CHUNKS * BLOCKS and (part == "M" or (part == "m") == (k == 0)):
+                            gate_block(gate_job)
+                if part == "P" and 0 <= step + 1 < N_STEPS:
+                    bank_numbers[step + 1] = list(free_banks[0:BACK_BANKS])
+                    project(HALVES * (step + 1))
+                    project(HALVES * (step + 1) + 1)
+                if part == "G" and 0 <= step + 1 < N_STEPS:
+                    turn_gate(HALVES * (step + 1))
+                    turn_gate(HALVES * (step + 1) + 1)

@@ -37,6 +37,7 @@ LOW_LEAD = GATE_LEAD + 1
 QUANT_LEAD = 1
 BACK_BANKS = 4
 POOL_TILES = 2
+POOL_STRIDE = 2
 ALL_POOL_FROM = 27
 ALL_POOL_TO = 30
 HEAD_HELP = (2, 2, 2, 2, 2, 2, 2, 2)
@@ -196,13 +197,13 @@ def tile_full_tmix_params_pb_t_kernel(
             chunk, j, h = where(unit)
             if unit // HALVES >= ALL_POOL_FROM:
                 return whole_tile_on_gpsimd(unit // HALVES)
-            return h == 1 and j < POOL_TILES
+            return h == 1 and j % POOL_STRIDE == 0 and j // POOL_STRIDE < POOL_TILES
 
         def group_of(unit):
             chunk, j, h = where(unit)
             if whole_tile_on_gpsimd(unit // HALVES):
                 return ("tile", unit // HALVES), h
-            return ("chunk", chunk), j
+            return ("chunk", chunk), j // POOL_STRIDE
 
         def before_of(chunk, g):
             sequence, first = divmod(CHUNK * chunk, SEQ)
@@ -382,9 +383,12 @@ def tile_full_tmix_params_pb_t_kernel(
             kept = kept_tiles[group]
             kind, number = group
             if kind == "chunk":
-                vf_view = vf_tiles[number][:, 0:POOL_TILES, HALF : 2 * HALF]
-                rows = slice(CHUNK * number, CHUNK * number + P * POOL_TILES)
-                out_view = out_rows[rows, HALF : 2 * HALF].rearrange("(j p) c -> p j c", p=P)
+                tiles = slice(0, POOL_STRIDE * POOL_TILES, POOL_STRIDE)
+                vf_view = vf_tiles[number][:, tiles, HALF : 2 * HALF]
+                rows = slice(CHUNK * number, CHUNK * (number + 1))
+                out_view = out_rows[rows, HALF : 2 * HALF].rearrange("(j p) c -> p j c", p=P)[
+                    :, tiles, :
+                ]
                 kept_view = kept[:, 0:POOL_TILES, :]
             else:
                 vf_view = vf_tiles[number // TILES][:, number % TILES, :].rearrange(

@@ -115,6 +115,7 @@ def tile_full_tmix_params_pb_t_kernel(
         load_x(0)
         v2_sb = consts.tile([P, C], BF16)
         nc.sync.dma_start(out=v2_sb[:], in_=v2)
+        load_x(1)
         w_words = consts.tile([P, PASSES, 2 * C], U8, align_bytes=64)
         w_scales = consts.tile([P, PASSES, C], U8, align_bytes=64)
         nc.vector.memset(w_scales[:].bitcast(I32), 0)
@@ -122,12 +123,13 @@ def tile_full_tmix_params_pb_t_kernel(
             nc.sync.dma_start(
                 out=w_words[:, g, :].bitcast(I32), in_=Wv_words[g].bitcast(I32)
             )
-        for g in range(PASSES):
-            for quad in range(4):
-                nc.sync.dma_start(
-                    out=w_scales[32 * quad : 32 * quad + 4, g, :].bitcast(I32),
-                    in_=Wv_scales[g, 4 * quad : 4 * quad + 4, :].bitcast(I32),
-                )
+        for quad in range(4):
+            nc.sync.dma_start(
+                out=w_scales[32 * quad : 32 * quad + 4, :, :].bitcast(I32),
+                in_=Wv_scales[:, 4 * quad : 4 * quad + 4, :]
+                .rearrange("g r n -> r g n")
+                .bitcast(I32),
+            )
 
         ident_f32 = consts.tile([P, P], F32)
         make_identity(nc, ident_f32[:])
@@ -437,7 +439,7 @@ def tile_full_tmix_params_pb_t_kernel(
             for due, out_view, kept_view in pending_stores:
                 if due == step:
                     nc.sync.dma_start(out=out_view, in_=kept_view)
-            if (step + X_LEAD) % TILES == 0 and (step + X_LEAD) // TILES + 1 < N_CHUNKS:
+            if (step + X_LEAD) % TILES == 0 and 2 <= (step + X_LEAD) // TILES + 1 < N_CHUNKS:
                 load_x((step + X_LEAD) // TILES + 1)
             if step % TILES == 0 and 0 <= step // TILES + 1 < N_CHUNKS:
                 load_v_first(step // TILES + 1)

@@ -43,6 +43,8 @@ ALL_POOL_TO = 30
 HEAD_HELP = (2, 2, 2, 2, 2, 2, 2, 2)
 VECTOR_JOBS = ()
 FIRST_SUM_AFTER = 4
+WARM_FIRST = 6
+WARM_STEP = 2
 PE_ORDER = "XMPG"
 CHUNK_STORE_LAG = 3
 TILE_STORE_LAG = 1
@@ -135,6 +137,18 @@ def tile_full_tmix_params_pb_t_kernel(
         make_identity(nc, ident_f32[:])
         ident_bf = consts.tile([P, P], BF16)
         make_identity(nc, ident_bf[:])
+
+        idle_sb = consts.tile([P, HALF], BF16)
+        nc.vector.memset(idle_sb[:], 0.0)
+        idle_ps = psum_back.tile([P, HALF], F32, tag="back%d" % (BACK_BANKS - 1))
+
+        def idle_matmuls(count):
+            for number in range(count):
+                nc.tensor.matmul(
+                    out=idle_ps[:], lhsT=idle_sb[:, 0:P], rhs=idle_sb[:], start=True, stop=True
+                )
+
+        idle_matmuls(WARM_FIRST)
 
         warm = consts.tile([P, 1], F32)
         nc.vector.memset(warm[:], 0.0)
@@ -444,6 +458,8 @@ def tile_full_tmix_params_pb_t_kernel(
             if step % TILES == 0 and 0 <= step // TILES + 1 < N_CHUNKS:
                 load_v_first(step // TILES + 1)
 
+            if step < -1:
+                idle_matmuls(WARM_STEP)
             for part in PE_ORDER:
                 if part == "X":
                     scale_job = step + X_LEAD

@@ -168,6 +168,8 @@ def tile_full_tmix_params_pb_t_kernel(
 
         v0_ps = psum_prep.tile([P, P], BF16, tag="prep")
         nc.tensor.transpose(v0_ps[:], v0_rows[:], ident_bf[:])
+        v0_cols = consts.tile([P, BLOCKS], F32)
+        nc.vector.tensor_copy(out=v0_cols[:], in_=v0_ps[:, 0:BLOCKS])
         neg_v0_cols = consts.tile([P, BLOCKS], F32)
         nc.vector.tensor_scalar_mul(
             out=neg_v0_cols[:], in0=v0_ps[:, 0:BLOCKS], scalar1=-1.0
@@ -214,6 +216,9 @@ def tile_full_tmix_params_pb_t_kernel(
             if unit // HALVES >= ALL_POOL_FROM:
                 return whole_tile_on_gpsimd(unit // HALVES)
             return h == 1 and j % POOL_STRIDE == 0 and j // POOL_STRIDE < POOL_TILES
+
+        def holds_complement(chunk, h):
+            return any(on_gpsimd(UNITS * chunk + HALVES * j + h) for j in range(TILES))
 
         def group_of(unit):
             chunk, j, h = where(unit)
@@ -308,13 +313,22 @@ def tile_full_tmix_params_pb_t_kernel(
                 stop=True,
             )
             gate_t = gate_pool.tile([P, CHUNK], F32)
-            nc.scalar.activation(
-                out=gate_t[:],
-                in_=z_t[:],
-                func=ACT.Sigmoid,
-                bias=neg_v0_cols[:, b : b + 1],
-                scale=-1.0,
-            )
+            if holds_complement(chunk, b // (HALF // P)):
+                nc.scalar.activation(
+                    out=gate_t[:],
+                    in_=z_t[:],
+                    func=ACT.Sigmoid,
+                    bias=neg_v0_cols[:, b : b + 1],
+                    scale=-1.0,
+                )
+            else:
+                nc.scalar.activation(
+                    out=gate_t[:],
+                    in_=z_t[:],
+                    func=ACT.Sigmoid,
+                    bias=v0_cols[:, b : b + 1],
+                    scale=1.0,
+                )
             gate_t_tiles[(chunk, b)] = gate_t
 
         def turn_gate(unit):
@@ -367,7 +381,8 @@ def tile_full_tmix_params_pb_t_kernel(
 
         def apply_gate(unit):
             diff = diff_tiles[unit]
-            if on_gpsimd(unit):
+            chunk, j, h = where(unit)
+            if on_gpsimd(unit) or not holds_complement(chunk, h):
                 nc.vector.tensor_tensor(
                     out=diff, in0=diff, in1=gate_banks[unit][:], op=ALU.mult
                 )
@@ -386,7 +401,10 @@ def tile_full_tmix_params_pb_t_kernel(
             token_tile = unit // HALVES
             result = out_pool.tile([P, HALF], F32)
             nc.vector.tensor_tensor(
-                out=result[:], in0=p_banks[unit][:], in1=diff_tiles[unit], op=ALU.subtract
+                out=result[:],
+                in0=p_banks[unit][:],
+                in1=diff_tiles[unit],
+                op=(ALU.subtract if holds_complement(unit // UNITS, h) else ALU.add),
             )
             nc.sync.dma_start(
                 out=out_rows[

@@ -48,6 +48,7 @@ WARM_STEP = 2
 PE_ORDER = "XMPG"
 CHUNK_STORE_LAG = 3
 TILE_STORE_LAG = 1
+LAST_GROUP_LAG = 1
 
 FLOPS = 2 * TOKENS * C * C + 2 * TOKENS * P * C
 
@@ -432,8 +433,12 @@ def tile_full_tmix_params_pb_t_kernel(
                     "p (h c) -> p h c", h=HALVES
                 )
                 kept_view = kept[:, 0:HALVES, :]
-            nc.gpsimd.tensor_tensor(out=kept_view, in0=vf_view, in1=kept_view, op=ALU.subtract)
-            pending_stores.extend([(due, out_view, kept_view)])
+            result_view = kept_view
+            if group == ("chunk", N_CHUNKS - 2):
+                xv = xv_pool.tile([P, POOL_TILES, HALF], F32, align_bytes=64)
+                result_view = xv[:]
+            nc.gpsimd.tensor_tensor(out=result_view, in0=vf_view, in1=kept_view, op=ALU.subtract)
+            pending_stores.extend([(due, out_view, result_view)])
 
         def blend(step):
             low_unit, high_unit = HALVES * step, HALVES * step + 1
@@ -457,16 +462,12 @@ def tile_full_tmix_params_pb_t_kernel(
                 quantise(quant_chunk)
                 if quant_chunk + 1 < N_CHUNKS:
                     mix_tokens(quant_chunk + 1, 0)
-                    if ("chunk", quant_chunk - 1) in kept_tiles:
-                        take_away(("chunk", quant_chunk - 1), step + CHUNK_STORE_LAG)
+                if ("chunk", quant_chunk - 1) in kept_tiles:
+                    take_away(("chunk", quant_chunk - 1), step + LAST_GROUP_LAG if quant_chunk + 1 == N_CHUNKS else step + CHUNK_STORE_LAG)
             if 0 <= step < N_STEPS:
                 blend(step)
                 if whole_tile_on_gpsimd(step):
                     take_away(("tile", step), step + TILE_STORE_LAG)
-                    if step == ALL_POOL_FROM:
-                        for late_chunk in (N_CHUNKS - 2, N_CHUNKS - 1):
-                            if ("chunk", late_chunk) in kept_tiles:
-                                take_away(("chunk", late_chunk), step + TILE_STORE_LAG)
 
             for due, out_view, kept_view in pending_stores:
                 if due == step:

@@ -274,10 +274,10 @@ def tile_full_tmix_params_pb_t_kernel(
             before, first = before_of(chunk, g)
             engine = nc.vector if (chunk == 0 and g == PASSES - 1) else nc.gpsimd
             engine.tensor_tensor(
-                out=xv[:, g, :, :].rearrange("p (c i) t -> p c t i", i=4),
-                in0=own_tiles[(chunk, g)][:].rearrange("p t (c i) -> p c t i", i=4),
+                out=xv[:, g, :, :].rearrange("p (c i) t -> p c t i", i=8),
+                in0=own_tiles[(chunk, g)][:].rearrange("p t (c i) -> p c t i", i=8),
                 in1=before[:, :, first : first + CHUNK].rearrange(
-                    "p t (c i) -> p c t i", i=4
+                    "p t (c i) -> p c t i", i=8
                 ),
                 op=ALU.add,
             )

from contextlib import ExitStack

import concourse.mybir as mybir
from concourse.masks import make_identity

F32 = mybir.dt.float32
BF16 = mybir.dt.bfloat16
I32 = mybir.dt.int32
U8 = mybir.dt.uint8
U32 = mybir.dt.uint32
FP8X4 = mybir.dt.float8_e4m3fn_x4
FP4X4 = mybir.dt.float4_e2m1fn_x4
ALU = mybir.AluOpType
ACT = mybir.ActivationFunctionType

P = 128
TOKENS = 4096
SEQ = 1024
C = 1024
PACK = 4
K_PASS = P * PACK
PASSES = C // K_PASS
CHUNK = 512
N_CHUNKS = TOKENS // CHUNK
TILES = CHUNK // P
HALF = 512
HALVES = C // HALF
N_UNITS = TOKENS // P * HALVES
UNITS = TILES * HALVES
BLOCKS = C // P
SCALE_JOBS = 2 * PASSES

N_STEPS = TOKENS // P
X_LEAD = 7
GATE_LEAD = 5
LOW_LEAD = GATE_LEAD + 1
QUANT_LEAD = 1
BACK_BANKS = 4
POOL_TILES = 2
POOL_STRIDE = 2
ALL_POOL_FROM = 27
ALL_POOL_TO = 30
HEAD_HELP = (2, 2, 2, 2, 2, 2, 2, 2)
VECTOR_JOBS = ()
FIRST_SUM_AFTER = 4
WARM_FIRST = 6
WARM_STEP = 2
PE_ORDER = "XMPG"
CHUNK_STORE_LAG = 3
TILE_STORE_LAG = 1
LAST_GROUP_LAG = 1

FLOPS = 2 * TOKENS * C * C + 2 * TOKENS * P * C


def tile_full_tmix_params_pb_t_kernel(
    tc, x, v_first, x_v, Wv_words, Wv_scales, v0, xv_v1, v2, out
):
    nc = tc.nc
    x_rows = x.flatten_outer_dims()
    vf_rows = v_first.flatten_outer_dims()
    low_rows = xv_v1.flatten_outer_dims()
    out_rows = out.flatten_outer_dims()

    with ExitStack() as stack:
        consts = stack.enter_context(tc.tile_pool(name="consts", bufs=1))
        x_pool = stack.enter_context(tc.tile_pool(name="x", bufs=2))
        vf_pool = stack.enter_context(tc.tile_pool(name="vf", bufs=3))
        low_pool = stack.enter_context(tc.tile_pool(name="low", bufs=2))
        own_pool = stack.enter_context(tc.tile_pool(name="own", bufs=3))
        xv_pool = stack.enter_context(tc.tile_pool(name="xv", bufs=1))
        code_pool = stack.enter_context(tc.tile_pool(name="codes", bufs=2))
        gate_pool = stack.enter_context(tc.tile_pool(name="gate", bufs=16))
        diff_pool = stack.enter_context(tc.tile_pool(name="diff", bufs=4))
        kept_pool = stack.enter_context(tc.tile_pool(name="kept", bufs=4))
        out_pool = stack.enter_context(tc.tile_pool(name="out", bufs=5))
        psum_prep = stack.enter_context(tc.psum_pool(name="psum_prep", bufs=4))
        psum_back = stack.enter_context(tc.psum_pool(name="psum_back", bufs=1))
        stack.enter_context(tc.manual_schedule())

        x_tiles = {}
        low_tiles = {}
        vf_tiles = {}

        def load_x(chunk):
            rows = slice(CHUNK * chunk, CHUNK * (chunk + 1))
            x_sb = x_pool.tile([P, TILES, C], BF16)
            for g in range(PASSES):
                channels = slice(K_PASS * g, K_PASS * (g + 1))
                nc.sync.dma_start(
                    out=x_sb[:, :, channels],
                    in_=x_rows[rows, channels].rearrange("(j p) c -> p j c", p=P),
                )
            x_tiles[chunk] = x_sb
            low_sb = low_pool.tile([P, TILES, P], BF16)
            nc.sync.dma_start(
                out=low_sb[:], in_=low_rows[rows, :].rearrange("(j p) d -> p j d", p=P)
            )
            low_tiles[chunk] = low_sb

        def load_v_first(chunk):
            rows = slice(CHUNK * chunk, CHUNK * (chunk + 1))
            vf_sb = vf_pool.tile([P, TILES, C], BF16)
            nc.sync.dma_start(
                out=vf_sb[:], in_=vf_rows[rows, :].rearrange("(j p) c -> p j c", p=P)
            )
            vf_tiles[chunk] = vf_sb

        mix_bf = consts.tile([P, PASSES, PACK], BF16)
        nc.sync.dma_start(
            out=mix_bf[:], in_=x_v.rearrange("(g p t) -> p g t", g=PASSES, p=P)
        )
        v0_rows = consts.tile([P, P], BF16)
        nc.vector.memset(v0_rows[:], 0.0)
        nc.sync.dma_start(
            out=v0_rows[0:BLOCKS, :], in_=v0.rearrange("(r c) -> r c", c=P)
        )
        load_x(0)
        v2_sb = consts.tile([P, C], BF16)
        nc.sync.dma_start(out=v2_sb[:], in_=v2)
        load_x(1)
        w_words = consts.tile([P, PASSES, 2 * C], U8, align_bytes=64)
        w_scales = consts.tile([P, PASSES, C], U8, align_bytes=64)
        nc.vector.memset(w_scales[:].bitcast(I32), 0)
        for g in range(PASSES):
            nc.sync.dma_start(
                out=w_words[:, g, :].bitcast(I32), in_=Wv_words[g].bitcast(I32)
            )
        for quad in range(4):
            nc.sync.dma_start(
                out=w_scales[32 * quad : 32 * quad + 4, :, :].bitcast(I32),
                in_=Wv_scales[:, 4 * quad : 4 * quad + 4, :]
                .rearrange("g r n -> r g n")
                .bitcast(I32),
            )

        ident_f32 = consts.tile([P, P], F32)
        make_identity(nc, ident_f32[:])
        ident_bf = consts.tile([P, P], BF16)
        make_identity(nc, ident_bf[:])

        idle_sb = consts.tile([P, HALF], BF16)
        nc.vector.memset(idle_sb[:], 0.0)
        idle_ps = psum_back.tile([P, HALF], F32, tag="back%d" % (BACK_BANKS - 1))

        def idle_matmuls(count):
            for number in range(count):
                nc.tensor.matmul(
                    out=idle_ps[:], lhsT=idle_sb[:, 0:P], rhs=idle_sb[:], start=True, stop=True
                )

        idle_matmuls(WARM_FIRST)

        warm = consts.tile([P, 1], F32)
        nc.vector.memset(warm[:], 0.0)
        nc.scalar.activation(out=warm[:], in_=warm[:], func=ACT.Sigmoid)

        mix = consts.tile([P, PASSES * PACK], F32)
        nc.vector.tensor_copy(out=mix[:], in_=mix_bf[:].rearrange("p g t -> p (g t)"))
        one_minus_mix = consts.tile([P, PASSES * PACK], F32)
        nc.vector.tensor_scalar(
            out=one_minus_mix[:],
            in0=mix_bf[:].rearrange("p g t -> p (g t)"),
            scalar1=-1.0,
            scalar2=1.0,
            op0=ALU.mult,
            op1=ALU.add,
        )

        v0_ps = psum_prep.tile([P, P], BF16, tag="prep")
        nc.tensor.transpose(v0_ps[:], v0_rows[:], ident_bf[:])
        v0_cols = consts.tile([P, BLOCKS], F32)
        nc.vector.tensor_copy(out=v0_cols[:], in_=v0_ps[:, 0:BLOCKS])
        neg_v0_cols = consts.tile([P, BLOCKS], F32)
        nc.vector.tensor_scalar_mul(
            out=neg_v0_cols[:], in0=v0_ps[:, 0:BLOCKS], scalar1=-1.0
        )

        zeros = consts.tile([P, PACK], F32)
        nc.vector.memset(zeros[:], 0.0)
        before_tiles = {}
        for parity in range(2):
            for g in range(PASSES):
                before = consts.tile(
                    [P, PACK, SEQ + PACK], F32, name="before_%d_%d" % (parity, g)
                )
                nc.scalar.copy(out=before[:, :, 0], in_=zeros[:])
                before_tiles[(parity, g)] = before

        own_tiles = {}
        xv_tiles = {}
        code_tiles = {}
        scale_tiles = {}
        low_t_tiles = {}
        gate_t_tiles = {}
        gate_banks = {}
        p_banks = {}
        diff_tiles = {}
        kept_tiles = {}
        bank_numbers = {}
        free_banks = list(range(BACK_BANKS))
        pending_stores = []

        def take_bank():
            bank = free_banks[0]
            free_banks.remove(bank)
            return bank

        def where(unit):
            return unit // UNITS, (unit % UNITS) // HALVES, unit % HALVES

        def whole_tile_on_gpsimd(step):
            return ALL_POOL_FROM <= step < ALL_POOL_TO

        def on_gpsimd(unit):
            chunk, j, h = where(unit)
            if unit // HALVES >= ALL_POOL_FROM:
                return whole_tile_on_gpsimd(unit // HALVES)
            return h == 1 and j % POOL_STRIDE == 0 and j // POOL_STRIDE < POOL_TILES

        def holds_complement(chunk, h):
            return any(on_gpsimd(UNITS * chunk + HALVES * j + h) for j in range(TILES))

        def group_of(unit):
            chunk, j, h = where(unit)
            if whole_tile_on_gpsimd(unit // HALVES):
                return ("tile", unit // HALVES), h
            return ("chunk", chunk), j // POOL_STRIDE

        def before_of(chunk, g):
            sequence, first = divmod(CHUNK * chunk, SEQ)
            return before_tiles[(sequence % 2, g)], first

        def scale_x(job, on_vector):
            chunk, g, u = job // SCALE_JOBS, (job % SCALE_JOBS) // 2, job % 2
            if u == 0:
                own = own_pool.tile([P, PACK, CHUNK], F32)
                own_tiles[(chunk, g)] = own
            own = own_tiles[(chunk, g)]
            before, first = before_of(chunk, g)
            x_t = psum_prep.tile([P, CHUNK], F32, tag="prep")
            for j in range(TILES):
                words = x_tiles[chunk][:, j, :].bitcast(F32)
                nc.tensor.transpose(
                    x_t[:, P * j : P * (j + 1)],
                    words[:, 256 * g + u : 256 * (g + 1) : 2],
                    ident_f32[:],
                )
            pairs = x_t[:].bitcast(BF16).rearrange("p (r e) -> p r e", e=2)
            scalings = []
            for e in range(2):
                t = 2 * u + e
                col = PACK * g + t
                scalings.extend(
                    [(before[:, t, first + 1 : first + 1 + CHUNK], e, mix[:, col : col + 1])]
                )
            for e in range(2):
                t = 2 * u + e
                col = PACK * g + t
                scalings.extend([(own[:, t, :], e, one_minus_mix[:, col : col + 1])])
            for number, (target, e, factor) in enumerate(scalings):
                if number >= len(scalings) - on_vector:
                    nc.vector.tensor_scalar_mul(out=target, in0=pairs[:, :, e], scalar1=factor)
                else:
                    nc.scalar.activation(
                        out=target, in_=pairs[:, :, e], func=ACT.Copy, scale=factor
                    )

        def mix_tokens(chunk, g):
            if g == 0:
                xv = xv_pool.tile([P, PASSES, CHUNK, PACK], BF16, align_bytes=64)
                xv_tiles[chunk] = xv
            xv = xv_tiles[chunk]
            before, first = before_of(chunk, g)
            engine = nc.vector if (chunk == 0 and g == PASSES - 1) else nc.gpsimd
            engine.tensor_tensor(
                out=xv[:, g, :, :].rearrange("p (c i) t -> p c t i", i=8),
                in0=own_tiles[(chunk, g)][:].rearrange("p t (c i) -> p c t i", i=8),
                in1=before[:, :, first : first + CHUNK].rearrange(
                    "p t (c i) -> p c t i", i=8
                ),
                op=ALU.add,
            )

        def quantise(chunk):
            codes = code_pool.tile([P, PASSES, CHUNK], U32, align_bytes=64)
            scales = code_pool.tile([P, PASSES, CHUNK], U8, align_bytes=64)
            nc.vector.quantize_mx(
                out=codes[:].rearrange("p g r -> p (g r)").bitcast(FP8X4),
                scales=scales[:].rearrange("p g r -> p (g r)"),
                in_=xv_tiles[chunk][:].rearrange("p g r t -> p (g r t)"),
            )
            code_tiles[chunk] = codes
            scale_tiles[chunk] = scales

        def turn_low_rank(chunk):
            low_ps = psum_prep.tile([P, CHUNK], BF16, tag="prep")
            for j in range(TILES):
                nc.tensor.transpose(
                    low_ps[:, P * j : P * (j + 1)], low_tiles[chunk][:, j, :], ident_bf[:]
                )
            low_t = low_pool.tile([P, CHUNK], BF16)
            nc.scalar.copy(out=low_t[:], in_=low_ps[:])
            low_t_tiles[chunk] = low_t

        def gate_block(job):
            chunk, b = job // BLOCKS, job % BLOCKS
            z_t = psum_prep.tile([P, CHUNK], F32, tag="prep")
            nc.tensor.matmul(
                out=z_t[:],
                lhsT=v2_sb[:, P * b : P * (b + 1)],
                rhs=low_t_tiles[chunk][:],
                start=True,
                stop=True,
            )
            gate_t = gate_pool.tile([P, CHUNK], F32)
            if holds_complement(chunk, b // (HALF // P)):
                nc.scalar.activation(
                    out=gate_t[:],
                    in_=z_t[:],
                    func=ACT.Sigmoid,
                    bias=neg_v0_cols[:, b : b + 1],
                    scale=-1.0,
                )
            else:
                nc.scalar.activation(
                    out=gate_t[:],
                    in_=z_t[:],
                    func=ACT.Sigmoid,
                    bias=v0_cols[:, b : b + 1],
                    scale=1.0,
                )
            gate_t_tiles[(chunk, b)] = gate_t

        def turn_gate(unit):
            chunk, j, h = where(unit)
            gate = psum_back.tile([P, HALF], F32, tag="back%d" % take_bank())
            for q in range(HALF // P):
                nc.tensor.transpose(
                    gate[:, P * q : P * (q + 1)],
                    gate_t_tiles[(chunk, (HALF // P) * h + q)][:, P * j : P * (j + 1)],
                    ident_f32[:],
                )
            gate_banks[unit] = gate

        def project(unit):
            chunk, j, h = where(unit)
            p_ps = psum_back.tile([P, HALF], F32, tag="back%d" % take_bank())
            for g in range(PASSES):
                nc.tensor.matmul_mx(
                    out=p_ps[:],
                    lhsT=code_tiles[chunk][:, g, P * j : P * (j + 1)].bitcast(FP8X4),
                    lhsT_scale=scale_tiles[chunk][:, g, P * j : P * (j + 1)],
                    rhs=w_words[:, g, 2 * HALF * h : 2 * HALF * (h + 1)].bitcast(FP4X4),
                    rhs_scale=w_scales[:, g, HALF * h : HALF * (h + 1)],
                    start=(g == 0),
                    stop=(g == PASSES - 1),
                )
            p_banks[unit] = p_ps

        def subtract(unit):
            chunk, j, h = where(unit)
            if on_gpsimd(unit):
                group, place = group_of(unit)
                if group not in kept_tiles:
                    if group[0] == "tile" and group[1] % 2 == 1:
                        own = own_pool.tile([P, 2, HALF], F32)
                        kept_tiles[group] = own
                    else:
                        kept = kept_pool.tile([P, max(POOL_TILES, HALVES), HALF], F32)
                        kept_tiles[group] = kept
                diff_tiles[unit] = kept_tiles[group][:, place, :]
            else:
                diff = diff_pool.tile([P, HALF], F32)
                diff_tiles[unit] = diff[:]
            nc.vector.tensor_tensor(
                out=diff_tiles[unit],
                in0=vf_tiles[chunk][:, j, HALF * h : HALF * (h + 1)],
                in1=p_banks[unit][:],
                op=ALU.subtract,
            )

        def apply_gate(unit):
            diff = diff_tiles[unit]
            chunk, j, h = where(unit)
            if on_gpsimd(unit) or not holds_complement(chunk, h):
                nc.vector.tensor_tensor(
                    out=diff, in0=diff, in1=gate_banks[unit][:], op=ALU.mult
                )
            else:
                nc.vector.scalar_tensor_tensor(
                    out=diff,
                    in0=gate_banks[unit][:],
                    scalar=1.0,
                    in1=diff,
                    op0=ALU.subtract,
                    op1=ALU.mult,
                )

        def add_back(unit):
            h = unit % HALVES
            token_tile = unit // HALVES
            result = out_pool.tile([P, HALF], F32)
            nc.vector.tensor_tensor(
                out=result[:],
                in0=p_banks[unit][:],
                in1=diff_tiles[unit],
                op=(ALU.subtract if holds_complement(unit // UNITS, h) else ALU.add),
            )
            nc.sync.dma_start(
                out=out_rows[
                    P * token_tile : P * (token_tile + 1), HALF * h : HALF * (h + 1)
                ],
                in_=result[:],
            )

        def take_away(group, due):
            kept = kept_tiles[group]
            kind, number = group
            if kind == "chunk":
                tiles = slice(0, POOL_STRIDE * POOL_TILES, POOL_STRIDE)
                vf_view = vf_tiles[number][:, tiles, HALF : 2 * HALF]
                rows = slice(CHUNK * number, CHUNK * (number + 1))
                out_view = out_rows[rows, HALF : 2 * HALF].rearrange("(j p) c -> p j c", p=P)[
                    :, tiles, :
                ]
                kept_view = kept[:, 0:POOL_TILES, :]
            else:
                vf_view = vf_tiles[number // TILES][:, number % TILES, :].rearrange(
                    "p (h c) -> p h c", h=HALVES
                )
                out_view = out_rows[P * number : P * (number + 1), :].rearrange(
                    "p (h c) -> p h c", h=HALVES
                )
                kept_view = kept[:, 0:HALVES, :]
            result_view = kept_view
            if group == ("chunk", N_CHUNKS - 2):
                xv = xv_pool.tile([P, POOL_TILES, HALF], F32, align_bytes=64)
                result_view = xv[:]
            nc.gpsimd.tensor_tensor(out=result_view, in0=vf_view, in1=kept_view, op=ALU.subtract)
            pending_stores.extend([(due, out_view, result_view)])

        def blend(step):
            low_unit, high_unit = HALVES * step, HALVES * step + 1
            banks = bank_numbers[step]
            subtract(low_unit)
            subtract(high_unit)
            apply_gate(low_unit)
            apply_gate(high_unit)
            for unit, bank in ((low_unit, banks[0]), (high_unit, banks[1])):
                if on_gpsimd(unit):
                    free_banks.extend([bank])
            free_banks.extend(banks[2:4])
            for unit, bank in ((low_unit, banks[0]), (high_unit, banks[1])):
                if not on_gpsimd(unit):
                    add_back(unit)
                    free_banks.extend([bank])

        for step in range(-X_LEAD, N_STEPS + max(CHUNK_STORE_LAG, TILE_STORE_LAG) + 1):
            quant_chunk, at_chunk_start = divmod(step + QUANT_LEAD, TILES)
            if at_chunk_start == 0 and 1 <= quant_chunk < N_CHUNKS:
                quantise(quant_chunk)
                if quant_chunk + 1 < N_CHUNKS:
                    mix_tokens(quant_chunk + 1, 0)
                if ("chunk", quant_chunk - 1) in kept_tiles:
                    take_away(("chunk", quant_chunk - 1), step + LAST_GROUP_LAG if quant_chunk + 1 == N_CHUNKS else step + CHUNK_STORE_LAG)
            if 0 <= step < N_STEPS:
                blend(step)
                if whole_tile_on_gpsimd(step):
                    take_away(("tile", step), step + TILE_STORE_LAG)

            for due, out_view, kept_view in pending_stores:
                if due == step:
                    nc.sync.dma_start(out=out_view, in_=kept_view)
            if (step + X_LEAD) % TILES == 0 and 2 <= (step + X_LEAD) // TILES + 1 < N_CHUNKS:
                load_x((step + X_LEAD) // TILES + 1)
            if step % TILES == 0 and 0 <= step // TILES + 1 < N_CHUNKS:
                load_v_first(step // TILES + 1)

            if step < -1:
                idle_matmuls(WARM_STEP)
            for part in PE_ORDER:
                if part == "X":
                    scale_job = step + X_LEAD
                    if scale_job < N_CHUNKS * SCALE_JOBS:
                        if step < 0:
                            on_vector = HEAD_HELP[scale_job]
                        else:
                            on_vector = 1 if scale_job % SCALE_JOBS in VECTOR_JOBS else 0
                        scale_x(scale_job, on_vector)
                        job_chunk, job_in_chunk = divmod(scale_job, SCALE_JOBS)
                        if job_chunk <= 1 and job_in_chunk == 1:
                            mix_tokens(job_chunk, 0)
                        if job_in_chunk == SCALE_JOBS - 1 and job_chunk > 0:
                            mix_tokens(job_chunk, 1)
                        if scale_job == FIRST_SUM_AFTER:
                            mix_tokens(0, 1)
                            quantise(0)
                    if (step + LOW_LEAD) % TILES == 0 and 0 <= (step + LOW_LEAD) // TILES < N_CHUNKS:
                        turn_low_rank((step + LOW_LEAD) // TILES)
                if part in ("M", "m", "n"):
                    for k in range(2):
                        gate_job = 2 * (step + GATE_LEAD) + k
                        if 0 <= gate_job < N_CHUNKS * BLOCKS and (part == "M" or (part == "m") == (k == 0)):
                            gate_block(gate_job)
                if part == "P" and 0 <= step + 1 < N_STEPS:
                    bank_numbers[step + 1] = list(free_banks[0:BACK_BANKS])
                    project(HALVES * (step + 1))
                    project(HALVES * (step + 1) + 1)
                if part == "G" and 0 <= step + 1 < N_STEPS:
                    turn_gate(HALVES * (step + 1))
                    turn_gate(HALVES * (step + 1) + 1)
